import numpy as np
import ml_dtypes


def mxq(x, axis, fmt="e4m3"):
    dtype, down = {"e4m3": (ml_dtypes.float8_e4m3fn, 7), "e5m2": (ml_dtypes.float8_e5m2, 14)}[fmt]
    v = np.moveaxis(np.asarray(x, np.float32).astype(ml_dtypes.bfloat16).astype(np.float64), axis, -1)
    blocks = v.reshape(v.shape[:-1] + (-1, 32))
    amax = np.abs(blocks).max(-1, keepdims=True)
    byte = np.maximum(np.where(amax > 0, np.frexp(amax)[1] - 1 + 127, 0) - down, 1)
    scale = np.exp2(byte - 127.0)
    codes = (blocks / scale).astype(np.float32).astype(dtype).astype(np.float64)
    return np.moveaxis((codes * scale).reshape(v.shape), -1, axis)


WIDE = False


def mx_kscale(k):
    if not WIDE:
        return np.ones(k)
    levels = np.array([10, -10, 5, -5, 0])
    a = np.random.permutation(np.resize(levels, k // 512 * 4)).reshape(k // 512, 4)
    idx = np.arange(k)
    return np.exp2(a[idx // 512, idx % 128 // 32])


BF16 = ml_dtypes.bfloat16


def bf(x):
    return np.asarray(x, np.float32).astype(BF16)


def f64(x):
    return np.asarray(x).astype(np.float64)


B, T, D, NH, N_MLP = 4, 128, 1024, 16, 4096
HD = D // NH
LN_EPS = 1e-6


def layer_norm(v, g, b):
    mu = v.mean(-1, keepdims=True)
    var = np.square(v - mu).mean(-1, keepdims=True)
    return (v - mu) / np.sqrt(var + LN_EPS) * g + b


def setup_inputs():
    s = mx_kscale(D)
    return {"x": bf(np.random.standard_normal((B, T, D)) * 1.5 + np.random.standard_normal((B, T, 1)) * 0.5),
            "W_qkv": bf(np.random.standard_normal((3 * D, D)) / np.sqrt(D) / s),
            "b_qkv": bf(np.random.standard_normal(3 * D) * 0.2),
            "g1": bf((1.0 + 0.1 * np.random.standard_normal(D)) * s),
            "beta1": bf(0.1 * np.random.standard_normal(D) * s)}


def reference(x, W_qkv, b_qkv, g1, beta1):
    h = layer_norm(f64(x), f64(g1), f64(beta1))
    qkv = (mxq(h, 2, "e4m3") @ mxq(f64(W_qkv), 1, "e4m3").T) + f64(b_qkv)
    qkv = qkv.reshape(B, T, 3, NH, HD)
    return qkv[:, :, 0].copy(), qkv[:, :, 1].copy(), qkv[:, :, 2].copy()

@@ -1,0 +1,240 @@
+from contextlib import ExitStack
+
+import concourse.mybir as mybir
+from concourse.masks import make_identity
+
+F32 = mybir.dt.float32
+BF16 = mybir.dt.bfloat16
+U32 = mybir.dt.uint32
+U8 = mybir.dt.uint8
+FP8X4 = mybir.dt.float8_e4m3fn_x4
+ACT = mybir.ActivationFunctionType
+ALU = mybir.AluOpType
+
+P = 128
+TOKENS = 512
+D = 1024
+FEATURES = 3 * D
+LN_EPS = 1e-6
+
+PACK = 4
+K_PASS = P * PACK
+PASSES = D // K_PASS
+PAIR = 2
+K_BLOCK = P * PAIR
+K_BLOCKS = D // K_BLOCK
+
+TOKEN_TILES = TOKENS // P
+TOKEN_GROUP = 2 * P
+TOKEN_GROUPS = TOKENS // TOKEN_GROUP
+
+CHUNK = 512
+CHUNKS = FEATURES // CHUNK
+ROW_TILES = CHUNK // P
+AHEAD = 2
+
+BN_WIDTH = 512
+BN_OUT = 6
+
+FLOPS = 2 * TOKENS * D * FEATURES
+
+
+def tile_block_pa_kernel(tc, x, W_qkv, b_qkv, g1, beta1, out_0, out_1, out_2):
+    nc = tc.nc
+    x_rows = x.flatten_outer_dims()
+    out_rows = [o.rearrange("b t h d -> (b t) (h d)") for o in (out_0, out_1, out_2)]
+
+    with ExitStack() as ctx:
+        keep = ctx.enter_context(tc.tile_pool(name="keep", bufs=1))
+        small = ctx.enter_context(tc.tile_pool(name="small", bufs=TOKEN_TILES))
+        normed = ctx.enter_context(tc.tile_pool(name="normed", bufs=TOKEN_TILES))
+        grouped = ctx.enter_context(tc.tile_pool(name="grouped", bufs=4))
+        results = ctx.enter_context(tc.tile_pool(name="results", bufs=8))
+        flip_banks = ctx.enter_context(tc.psum_pool(name="flip_banks", bufs=4))
+        sum_banks = ctx.enter_context(tc.psum_pool(name="sum_banks", bufs=4))
+
+        x_sb = keep.tile([P, TOKEN_TILES, D], BF16)
+        for i in range(TOKEN_TILES):
+            nc.sync.dma_start(out=x_sb[:, i, :], in_=x_rows[i * P : (i + 1) * P, :])
+        w_sb = keep.tile([P, CHUNKS, ROW_TILES, D], BF16)
+        for c in range(CHUNKS):
+            nc.sync.dma_start(
+                out=w_sb[:, c, :, :],
+                in_=W_qkv[c * CHUNK : (c + 1) * CHUNK, :].rearrange("(r p) k -> p r k", p=P),
+            )
+        w_words = w_sb[:].bitcast(F32)
+
+        gain_rows = keep.tile([P, K_BLOCK], BF16)
+        nc.vector.memset(gain_rows[:], 0.0)
+        nc.scalar.dma_start(
+            out=gain_rows[0:K_BLOCKS, :], in_=g1.rearrange("(r c) -> r c", c=K_BLOCK)
+        )
+        nc.scalar.dma_start(
+            out=gain_rows[K_BLOCKS : 2 * K_BLOCKS, :],
+            in_=beta1.rearrange("(r c) -> r c", c=K_BLOCK),
+        )
+        bias_rows = keep.tile([P, CHUNK], BF16)
+        nc.vector.memset(bias_rows[:], 0.0)
+        nc.scalar.dma_start(
+            out=bias_rows[0:CHUNKS, :], in_=b_qkv.rearrange("(r c) -> r c", c=CHUNK)
+        )
+
+        eps_col = keep.tile([P, 1], F32)
+        nc.vector.memset(eps_col[:], LN_EPS)
+        table_warmer = keep.tile([P, 1], F32)
+        nc.scalar.activation(out=table_warmer[:], in_=eps_col[:], func=ACT.Sqrt)
+        ident_f32 = keep.tile([P, P], F32)
+        make_identity(nc, ident_f32[:])
+        ident_bf16 = keep.tile([P, P], BF16)
+        make_identity(nc, ident_bf16[:])
+
+        gain_flipped = flip_banks.tile([P, P], F32, tag="flip")
+        nc.tensor.transpose(gain_flipped[:], gain_rows[:].bitcast(F32), ident_f32[:])
+        gain_pairs = keep.tile([P, 2 * K_BLOCKS], F32)
+        nc.vector.tensor_copy(out=gain_pairs[:], in_=gain_flipped[:, 0 : 2 * K_BLOCKS])
+        gain_cols = keep.tile([P, 2 * K_BLOCKS * PAIR], F32)
+        nc.vector.tensor_copy(out=gain_cols[:], in_=gain_pairs[:].bitcast(BF16))
+        beta_at = K_BLOCKS * PAIR
+
+        bias_all = keep.tile([P, FEATURES], BF16)
+        for b in range(CHUNKS // 2):
+            bias_bank = flip_banks.tile([P, 2 * CHUNK], BF16, tag="flip")
+            for half in range(2):
+                c = 2 * b + half
+                nc.tensor.matmul(
+                    out=bias_bank[:, half * CHUNK : (half + 1) * CHUNK],
+                    lhsT=ident_bf16[:, c : c + 1].to_broadcast([P, P]),
+                    rhs=bias_rows[:],
+                    start=True,
+                    stop=True,
+                )
+            nc.scalar.copy(out=bias_all[:, 2 * b * CHUNK : 2 * (b + 1) * CHUNK], in_=bias_bank[:])
+
+        h_codes = keep.tile([P, PASSES, TOKENS], U32, align_bytes=64)
+        h_scales = keep.tile([P, PASSES, TOKENS], U8, align_bytes=64)
+        w_codes = keep.tile([P, CHUNKS, PASSES, CHUNK], U32, align_bytes=64)
+        w_scales = keep.tile([P, CHUNKS, PASSES, CHUNK], U8, align_bytes=64)
+        h_planes = keep.tile([P, PASSES, PACK, TOKENS], BF16)
+        h_grouped = keep.tile([P, PASSES, TOKENS, PACK], BF16, align_bytes=64)
+
+        def normalise(i):
+            stats = small.tile([P, D // BN_WIDTH, BN_OUT], F32)
+            for s in range(D // BN_WIDTH):
+                nc.vector.bn_stats(
+                    out=stats[:, s, :], in_=x_sb[:, i, s * BN_WIDTH : (s + 1) * BN_WIDTH]
+                )
+            mean_var = small.tile([P, 2], F32)
+            nc.vector.bn_aggr(out=mean_var[:], in_=stats[:].rearrange("p s d -> p (s d)"))
+            std = small.tile([P, 1], F32)
+            nc.scalar.activation(out=std[:], in_=mean_var[:, 1:2], func=ACT.Sqrt, bias=eps_col[:])
+            rstd = small.tile([P, 1], F32)
+            nc.vector.reciprocal(out=rstd[:], in_=std[:])
+            shift = small.tile([P, 1], F32)
+            nc.vector.tensor_scalar(
+                out=shift[:],
+                in0=mean_var[:, 0:1],
+                scalar1=rstd[:],
+                scalar2=-1.0,
+                op0=ALU.mult,
+                op1=ALU.mult,
+            )
+            xn = normed.tile([P, PAIR, D // PAIR], F32)
+            nc.scalar.activation(
+                out=xn[:],
+                in_=x_sb[:, i, :].rearrange("p (j e) -> p e j", e=PAIR),
+                func=ACT.Identity,
+                scale=rstd[:],
+                bias=shift[:],
+            )
+            return xn
+
+        def quantise_h(group, xn_tiles):
+            tokens = slice(group * TOKEN_GROUP, (group + 1) * TOKEN_GROUP)
+            for b in range(K_BLOCKS):
+                g, u = divmod(b, 2)
+                flipped = sum_banks.tile([P, PAIR, TOKEN_GROUP], F32, tag="sum")
+                for r, xn in enumerate(xn_tiles):
+                    for e in range(PAIR):
+                        nc.tensor.transpose(
+                            flipped[:, e, r * P : (r + 1) * P],
+                            xn[:, e, b * P : (b + 1) * P],
+                            ident_f32[:],
+                        )
+                for e in range(PAIR):
+                    col = PAIR * b + e
+                    nc.scalar.activation(
+                        out=h_planes[:, g, PAIR * u + e, tokens],
+                        in_=flipped[:, e, :],
+                        func=ACT.Identity,
+                        scale=gain_cols[:, col : col + 1],
+                        bias=gain_cols[:, beta_at + col : beta_at + col + 1],
+                    )
+            for g in range(PASSES):
+                nc.vector.tensor_copy(
+                    out=h_grouped[:, g, tokens, :],
+                    in_=h_planes[:, g, :, tokens].rearrange("p t n -> p n t"),
+                )
+            for g in range(PASSES):
+                nc.vector.quantize_mx(
+                    out=h_codes[:, g, tokens].bitcast(FP8X4),
+                    scales=h_scales[:, g, tokens],
+                    in_=h_grouped[:, g, tokens, :].rearrange("p n t -> p (n t)"),
+                )
+
+        def prepare_weights(c):
+            for g in range(PASSES):
+                w_grouped = grouped.tile([P, CHUNK * PACK], BF16, align_bytes=64)
+                w_grouped_words = w_grouped[:].bitcast(F32).rearrange(
+                    "p (r f u) -> p r f u", r=ROW_TILES, u=2
+                )
+                for half in range(2):
+                    flipped = flip_banks.tile([P, 2, 2, P], F32, tag="flip")
+                    for r in range(2):
+                        for u in range(2):
+                            b = 2 * g + u
+                            nc.tensor.transpose(
+                                flipped[:, r, u, :],
+                                w_words[:, c, 2 * half + r, b * P : (b + 1) * P],
+                                ident_f32[:],
+                            )
+                    nc.scalar.copy(
+                        out=w_grouped_words[:, 2 * half : 2 * half + 2, :, :],
+                        in_=flipped[:].rearrange("p r u f -> p r f u"),
+                    )
+                nc.vector.quantize_mx(
+                    out=w_codes[:, c, g, :].bitcast(FP8X4),
+                    scales=w_scales[:, c, g, :],
+                    in_=w_grouped[:],
+                )
+
+        def multiply(c):
+            columns = slice((c % 2) * CHUNK, (c % 2 + 1) * CHUNK)
+            for i in range(TOKEN_TILES):
+                rows = slice(i * P, (i + 1) * P)
+                sums = sum_banks.tile([P, CHUNK], F32, tag="sum")
+                for g in range(PASSES):
+                    nc.tensor.matmul_mx(
+                        out=sums[:],
+                        lhsT=h_codes[:, g, rows].bitcast(FP8X4),
+                        lhsT_scale=h_scales[:, g, rows],
+                        rhs=w_codes[:, c, g, :].bitcast(FP8X4),
+                        rhs_scale=w_scales[:, c, g, :],
+                        start=(g == 0),
+                        stop=(g == PASSES - 1),
+                    )
+                result = results.tile([P, CHUNK], F32)
+                nc.vector.tensor_tensor(
+                    out=result[:],
+                    in0=sums[:],
+                    in1=bias_all[:, c * CHUNK : (c + 1) * CHUNK],
+                    op=ALU.add,
+                )
+                nc.sync.dma_start(out=out_rows[c // 2][rows, columns], in_=result[:])
+
+        for group in range(TOKEN_GROUPS):
+            quantise_h(group, [normalise(2 * group), normalise(2 * group + 1)])
+            prepare_weights(group)
+        for c in range(CHUNKS):
+            if c + AHEAD < CHUNKS:
+                prepare_weights(c + AHEAD)
+            multiply(c)

@@ -129,22 +129,16 @@ def tile_block_pa_kernel(tc, x, W_qkv, b_qkv, g1, beta1, out_0, out_1, out_2):
             nc.scalar.activation(out=std[:], in_=mean_var[:, 1:2], func=ACT.Sqrt, bias=eps_col[:])
             rstd = small.tile([P, 1], F32)
             nc.vector.reciprocal(out=rstd[:], in_=std[:])
-            shift = small.tile([P, 1], F32)
-            nc.vector.tensor_scalar(
-                out=shift[:],
-                in0=mean_var[:, 0:1],
-                scalar1=rstd[:],
-                scalar2=-1.0,
-                op0=ALU.mult,
-                op1=ALU.mult,
-            )
+            neg_mean = small.tile([P, 1], F32)
+            nc.vector.tensor_scalar_mul(out=neg_mean[:], in0=mean_var[:, 0:1], scalar1=-1.0)
             xn = normed.tile([P, PAIR, D // PAIR], F32)
-            nc.scalar.activation(
+            nc.gpsimd.tensor_scalar(
                 out=xn[:],
-                in_=x_sb[:, i, :].rearrange("p (j e) -> p e j", e=PAIR),
-                func=ACT.Identity,
-                scale=rstd[:],
-                bias=shift[:],
+                in0=x_sb[:, i, :].rearrange("p (j e) -> p e j", e=PAIR),
+                scalar1=neg_mean[:],
+                scalar2=rstd[:],
+                op0=ALU.add,
+                op1=ALU.mult,
             )
             return xn
 
@@ -162,13 +156,23 @@ def tile_block_pa_kernel(tc, x, W_qkv, b_qkv, g1, beta1, out_0, out_1, out_2):
                         )
                 for e in range(PAIR):
                     col = PAIR * b + e
-                    nc.scalar.activation(
-                        out=h_planes[:, g, PAIR * u + e, tokens],
-                        in_=flipped[:, e, :],
-                        func=ACT.Identity,
-                        scale=gain_cols[:, col : col + 1],
-                        bias=gain_cols[:, beta_at + col : beta_at + col + 1],
-                    )
+                    if b % 2 == 0:
+                        nc.scalar.activation(
+                            out=h_planes[:, g, PAIR * u + e, tokens],
+                            in_=flipped[:, e, :],
+                            func=ACT.Identity,
+                            scale=gain_cols[:, col : col + 1],
+                            bias=gain_cols[:, beta_at + col : beta_at + col + 1],
+                        )
+                    else:
+                        nc.vector.tensor_scalar(
+                            out=h_planes[:, g, PAIR * u + e, tokens],
+                            in0=flipped[:, e, :],
+                            scalar1=gain_cols[:, col : col + 1],
+                            scalar2=gain_cols[:, beta_at + col : beta_at + col + 1],
+                            op0=ALU.mult,
+                            op1=ALU.add,
+                        )
             for g in range(PASSES):
                 nc.vector.tensor_copy(
                     out=h_grouped[:, g, tokens, :],

@@ -25,13 +25,14 @@ K_BLOCK = P * PAIR
 K_BLOCKS = D // K_BLOCK
 
 TOKEN_TILES = TOKENS // P
-TOKEN_GROUP = 2 * P
+GROUP_TILES = 2
+TOKEN_GROUP = GROUP_TILES * P
 TOKEN_GROUPS = TOKENS // TOKEN_GROUP
 
 CHUNK = 512
 CHUNKS = FEATURES // CHUNK
 ROW_TILES = CHUNK // P
-AHEAD = 2
+BANK_ROW_TILES = 2
 
 BN_WIDTH = 512
 BN_OUT = 6
@@ -45,14 +46,24 @@ def tile_block_pa_kernel(tc, x, W_qkv, b_qkv, g1, beta1, out_0, out_1, out_2):
     out_rows = [o.rearrange("b t h d -> (b t) (h d)") for o in (out_0, out_1, out_2)]
 
     with ExitStack() as ctx:
+        ctx.enter_context(tc.manual_schedule())
         keep = ctx.enter_context(tc.tile_pool(name="keep", bufs=1))
         small = ctx.enter_context(tc.tile_pool(name="small", bufs=TOKEN_TILES))
         normed = ctx.enter_context(tc.tile_pool(name="normed", bufs=TOKEN_TILES))
-        grouped = ctx.enter_context(tc.tile_pool(name="grouped", bufs=4))
-        results = ctx.enter_context(tc.tile_pool(name="results", bufs=8))
+        grouped = ctx.enter_context(tc.tile_pool(name="grouped", bufs=2 * PASSES))
+        results = ctx.enter_context(tc.tile_pool(name="results", bufs=2 * TOKEN_TILES))
         flip_banks = ctx.enter_context(tc.psum_pool(name="flip_banks", bufs=4))
         sum_banks = ctx.enter_context(tc.psum_pool(name="sum_banks", bufs=4))
 
+        gain_rows = keep.tile([P, K_BLOCK], BF16)
+        nc.vector.memset(gain_rows[:], 0.0)
+        nc.sync.dma_start(
+            out=gain_rows[0:K_BLOCKS, :], in_=g1.rearrange("(r c) -> r c", c=K_BLOCK)
+        )
+        nc.sync.dma_start(
+            out=gain_rows[K_BLOCKS : 2 * K_BLOCKS, :],
+            in_=beta1.rearrange("(r c) -> r c", c=K_BLOCK),
+        )
         x_sb = keep.tile([P, TOKEN_TILES, D], BF16)
         for i in range(TOKEN_TILES):
             nc.sync.dma_start(out=x_sb[:, i, :], in_=x_rows[i * P : (i + 1) * P, :])
@@ -63,52 +74,14 @@ def tile_block_pa_kernel(tc, x, W_qkv, b_qkv, g1, beta1, out_0, out_1, out_2):
                 in_=W_qkv[c * CHUNK : (c + 1) * CHUNK, :].rearrange("(r p) k -> p r k", p=P),
             )
         w_words = w_sb[:].bitcast(F32)
-
-        gain_rows = keep.tile([P, K_BLOCK], BF16)
-        nc.vector.memset(gain_rows[:], 0.0)
-        nc.scalar.dma_start(
-            out=gain_rows[0:K_BLOCKS, :], in_=g1.rearrange("(r c) -> r c", c=K_BLOCK)
-        )
-        nc.scalar.dma_start(
-            out=gain_rows[K_BLOCKS : 2 * K_BLOCKS, :],
-            in_=beta1.rearrange("(r c) -> r c", c=K_BLOCK),
-        )
-        bias_rows = keep.tile([P, CHUNK], BF16)
-        nc.vector.memset(bias_rows[:], 0.0)
-        nc.scalar.dma_start(
-            out=bias_rows[0:CHUNKS, :], in_=b_qkv.rearrange("(r c) -> r c", c=CHUNK)
-        )
+        bias_all = keep.tile([P, FEATURES], BF16)
 
         eps_col = keep.tile([P, 1], F32)
         nc.vector.memset(eps_col[:], LN_EPS)
         table_warmer = keep.tile([P, 1], F32)
         nc.scalar.activation(out=table_warmer[:], in_=eps_col[:], func=ACT.Sqrt)
-        ident_f32 = keep.tile([P, P], F32)
-        make_identity(nc, ident_f32[:])
-        ident_bf16 = keep.tile([P, P], BF16)
-        make_identity(nc, ident_bf16[:])
-
-        gain_flipped = flip_banks.tile([P, P], F32, tag="flip")
-        nc.tensor.transpose(gain_flipped[:], gain_rows[:].bitcast(F32), ident_f32[:])
-        gain_pairs = keep.tile([P, 2 * K_BLOCKS], F32)
-        nc.vector.tensor_copy(out=gain_pairs[:], in_=gain_flipped[:, 0 : 2 * K_BLOCKS])
-        gain_cols = keep.tile([P, 2 * K_BLOCKS * PAIR], F32)
-        nc.vector.tensor_copy(out=gain_cols[:], in_=gain_pairs[:].bitcast(BF16))
-        beta_at = K_BLOCKS * PAIR
-
-        bias_all = keep.tile([P, FEATURES], BF16)
-        for b in range(CHUNKS // 2):
-            bias_bank = flip_banks.tile([P, 2 * CHUNK], BF16, tag="flip")
-            for half in range(2):
-                c = 2 * b + half
-                nc.tensor.matmul(
-                    out=bias_bank[:, half * CHUNK : (half + 1) * CHUNK],
-                    lhsT=ident_bf16[:, c : c + 1].to_broadcast([P, P]),
-                    rhs=bias_rows[:],
-                    start=True,
-                    stop=True,
-                )
-            nc.scalar.copy(out=bias_all[:, 2 * b * CHUNK : 2 * (b + 1) * CHUNK], in_=bias_bank[:])
+        ident = keep.tile([P, P], F32)
+        make_identity(nc, ident[:])
 
         h_codes = keep.tile([P, PASSES, TOKENS], U32, align_bytes=64)
         h_scales = keep.tile([P, PASSES, TOKENS], U8, align_bytes=64)
@@ -116,8 +89,17 @@ def tile_block_pa_kernel(tc, x, W_qkv, b_qkv, g1, beta1, out_0, out_1, out_2):
         w_scales = keep.tile([P, CHUNKS, PASSES, CHUNK], U8, align_bytes=64)
         h_planes = keep.tile([P, PASSES, PACK, TOKENS], BF16)
         h_grouped = keep.tile([P, PASSES, TOKENS, PACK], BF16, align_bytes=64)
+        gain_cols = keep.tile([P, 2 * K_BLOCKS * PAIR], F32)
+        beta_at = K_BLOCKS * PAIR
 
-        def normalise(i):
+        def spread_gains():
+            gain_flipped = flip_banks.tile([P, P], F32, tag="flip")
+            nc.tensor.transpose(gain_flipped[:], gain_rows[:].bitcast(F32), ident[:])
+            gain_pairs = keep.tile([P, 2 * K_BLOCKS], F32)
+            nc.vector.tensor_copy(out=gain_pairs[:], in_=gain_flipped[:, 0 : 2 * K_BLOCKS])
+            nc.vector.tensor_copy(out=gain_cols[:], in_=gain_pairs[:].bitcast(BF16))
+
+        def statistics(i):
             stats = small.tile([P, D // BN_WIDTH, BN_OUT], F32)
             for s in range(D // BN_WIDTH):
                 nc.vector.bn_stats(
@@ -125,12 +107,15 @@ def tile_block_pa_kernel(tc, x, W_qkv, b_qkv, g1, beta1, out_0, out_1, out_2):
                 )
             mean_var = small.tile([P, 2], F32)
             nc.vector.bn_aggr(out=mean_var[:], in_=stats[:].rearrange("p s d -> p (s d)"))
-            std = small.tile([P, 1], F32)
-            nc.scalar.activation(out=std[:], in_=mean_var[:, 1:2], func=ACT.Sqrt, bias=eps_col[:])
-            rstd = small.tile([P, 1], F32)
-            nc.vector.reciprocal(out=rstd[:], in_=std[:])
             neg_mean = small.tile([P, 1], F32)
             nc.vector.tensor_scalar_mul(out=neg_mean[:], in0=mean_var[:, 0:1], scalar1=-1.0)
+            std = small.tile([P, 1], F32)
+            nc.scalar.activation(out=std[:], in_=mean_var[:, 1:2], func=ACT.Sqrt, bias=eps_col[:])
+            return neg_mean, std
+
+        def normalise(i, neg_mean, std):
+            rstd = small.tile([P, 1], F32)
+            nc.vector.reciprocal(out=rstd[:], in_=std[:])
             xn = normed.tile([P, PAIR, D // PAIR], F32)
             nc.gpsimd.tensor_scalar(
                 out=xn[:],
@@ -142,37 +127,34 @@ def tile_block_pa_kernel(tc, x, W_qkv, b_qkv, g1, beta1, out_0, out_1, out_2):
             )
             return xn
 
-        def quantise_h(group, xn_tiles):
-            tokens = slice(group * TOKEN_GROUP, (group + 1) * TOKEN_GROUP)
+        def flip_h(banks, tag, xn_tiles):
+            flipped = []
             for b in range(K_BLOCKS):
-                g, u = divmod(b, 2)
-                flipped = sum_banks.tile([P, PAIR, TOKEN_GROUP], F32, tag="sum")
+                bank = banks.tile([P, PAIR, TOKEN_GROUP], F32, tag=tag)
                 for r, xn in enumerate(xn_tiles):
                     for e in range(PAIR):
                         nc.tensor.transpose(
-                            flipped[:, e, r * P : (r + 1) * P],
-                            xn[:, e, b * P : (b + 1) * P],
-                            ident_f32[:],
+                            bank[:, e, r * P : (r + 1) * P], xn[:, e, b * P : (b + 1) * P], ident[:]
                         )
+                flipped.append(bank)
+            return flipped
+
+        def scale_h(group, flipped):
+            tokens = slice(group * TOKEN_GROUP, (group + 1) * TOKEN_GROUP)
+            for b in range(K_BLOCKS):
+                g, u = divmod(b, 2)
                 for e in range(PAIR):
                     col = PAIR * b + e
-                    if b % 2 == 0:
-                        nc.scalar.activation(
-                            out=h_planes[:, g, PAIR * u + e, tokens],
-                            in_=flipped[:, e, :],
-                            func=ACT.Identity,
-                            scale=gain_cols[:, col : col + 1],
-                            bias=gain_cols[:, beta_at + col : beta_at + col + 1],
-                        )
-                    else:
-                        nc.vector.tensor_scalar(
-                            out=h_planes[:, g, PAIR * u + e, tokens],
-                            in0=flipped[:, e, :],
-                            scalar1=gain_cols[:, col : col + 1],
-                            scalar2=gain_cols[:, beta_at + col : beta_at + col + 1],
-                            op0=ALU.mult,
-                            op1=ALU.add,
-                        )
+                    nc.scalar.activation(
+                        out=h_planes[:, g, PAIR * u + e, tokens],
+                        in_=flipped[b][:, e, :],
+                        func=ACT.Identity,
+                        scale=gain_cols[:, col : col + 1],
+                        bias=gain_cols[:, beta_at + col : beta_at + col + 1],
+                    )
+
+        def pack_h(group):
+            tokens = slice(group * TOKEN_GROUP, (group + 1) * TOKEN_GROUP)
             for g in range(PASSES):
                 nc.vector.tensor_copy(
                     out=h_grouped[:, g, tokens, :],
@@ -185,35 +167,45 @@ def tile_block_pa_kernel(tc, x, W_qkv, b_qkv, g1, beta1, out_0, out_1, out_2):
                     in_=h_grouped[:, g, tokens, :].rearrange("p n t -> p (n t)"),
                 )
 
-        def prepare_weights(c):
-            for g in range(PASSES):
-                w_grouped = grouped.tile([P, CHUNK * PACK], BF16, align_bytes=64)
-                w_grouped_words = w_grouped[:].bitcast(F32).rearrange(
-                    "p (r f u) -> p r f u", r=ROW_TILES, u=2
-                )
-                for half in range(2):
-                    flipped = flip_banks.tile([P, 2, 2, P], F32, tag="flip")
-                    for r in range(2):
-                        for u in range(2):
-                            b = 2 * g + u
-                            nc.tensor.transpose(
-                                flipped[:, r, u, :],
-                                w_words[:, c, 2 * half + r, b * P : (b + 1) * P],
-                                ident_f32[:],
-                            )
-                    nc.scalar.copy(
-                        out=w_grouped_words[:, 2 * half : 2 * half + 2, :, :],
-                        in_=flipped[:].rearrange("p r u f -> p r f u"),
-                    )
-                nc.vector.quantize_mx(
-                    out=w_codes[:, c, g, :].bitcast(FP8X4),
-                    scales=w_scales[:, c, g, :],
-                    in_=w_grouped[:],
-                )
+        def flip_weights(c, g):
+            flipped = []
+            for half in range(ROW_TILES // BANK_ROW_TILES):
+                bank = flip_banks.tile([P, BANK_ROW_TILES, 2, P], F32, tag="flip")
+                for r in range(BANK_ROW_TILES):
+                    for u in range(2):
+                        b = 2 * g + u
+                        nc.tensor.transpose(
+                            bank[:, r, u, :],
+                            w_words[:, c, BANK_ROW_TILES * half + r, b * P : (b + 1) * P],
+                            ident[:],
+                        )
+                flipped.append(bank)
+            return flipped
 
-        def multiply(c):
-            columns = slice((c % 2) * CHUNK, (c % 2 + 1) * CHUNK)
-            for i in range(TOKEN_TILES):
+        def copy_weights(flipped):
+            w_grouped = grouped.tile([P, CHUNK * PACK], BF16, align_bytes=64)
+            w_grouped_words = w_grouped[:].bitcast(F32).rearrange(
+                "p (r f u) -> p r f u", r=ROW_TILES, u=2
+            )
+            for half, bank in enumerate(flipped):
+                nc.scalar.copy(
+                    out=w_grouped_words[
+                        :, BANK_ROW_TILES * half : BANK_ROW_TILES * (half + 1), :, :
+                    ],
+                    in_=bank[:].rearrange("p r u f -> p r f u"),
+                )
+            return w_grouped
+
+        def quantise_weights(c, g, w_grouped):
+            nc.vector.quantize_mx(
+                out=w_codes[:, c, g, :].bitcast(FP8X4),
+                scales=w_scales[:, c, g, :],
+                in_=w_grouped[:],
+            )
+
+        def multiply(c, tiles):
+            banks = []
+            for i in tiles:
                 rows = slice(i * P, (i + 1) * P)
                 sums = sum_banks.tile([P, CHUNK], F32, tag="sum")
                 for g in range(PASSES):
@@ -226,6 +218,12 @@ def tile_block_pa_kernel(tc, x, W_qkv, b_qkv, g1, beta1, out_0, out_1, out_2):
                         start=(g == 0),
                         stop=(g == PASSES - 1),
                     )
+                banks.append(sums)
+            return banks
+
+        def finish(c, tiles, banks):
+            columns = slice((c % 2) * CHUNK, (c % 2 + 1) * CHUNK)
+            for i, sums in zip(tiles, banks):
                 result = results.tile([P, CHUNK], F32)
                 nc.vector.tensor_tensor(
                     out=result[:],
@@ -233,12 +231,56 @@ def tile_block_pa_kernel(tc, x, W_qkv, b_qkv, g1, beta1, out_0, out_1, out_2):
                     in1=bias_all[:, c * CHUNK : (c + 1) * CHUNK],
                     op=ALU.add,
                 )
-                nc.sync.dma_start(out=out_rows[c // 2][rows, columns], in_=result[:])
+                nc.sync.dma_start(
+                    out=out_rows[c // 2][i * P : (i + 1) * P, columns], in_=result[:]
+                )
 
-        for group in range(TOKEN_GROUPS):
-            quantise_h(group, [normalise(2 * group), normalise(2 * group + 1)])
-            prepare_weights(group)
-        for c in range(CHUNKS):
-            if c + AHEAD < CHUNKS:
-                prepare_weights(c + AHEAD)
-            multiply(c)
+        def flip_and_copy_weights(c):
+            flipped = [flip_weights(c, g) for g in range(PASSES)]
+            return [copy_weights(banks) for banks in flipped]
+
+        group_tiles = [
+            list(range(q * GROUP_TILES, (q + 1) * GROUP_TILES)) for q in range(TOKEN_GROUPS)
+        ]
+        all_tiles = list(range(TOKEN_TILES))
+
+        moments = []
+        xn_tiles = []
+        ready = {}
+        ready[0] = []
+        for i in range(TOKEN_TILES):
+            moments.append(statistics(i))
+            if i >= 1:
+                xn_tiles.append(normalise(i - 1, *moments[i - 1]))
+            if i >= TOKEN_TILES - PASSES:
+                ready[0].append(copy_weights(flip_weights(0, i - (TOKEN_TILES - PASSES))))
+        xn_tiles.append(normalise(TOKEN_TILES - 1, *moments[TOKEN_TILES - 1]))
+        spread_gains()
+        nc.scalar.dma_start(out=bias_all[:], in_=b_qkv.partition_broadcast(P))
+        for g in range(PASSES):
+            quantise_weights(0, g, ready[0][g])
+
+        flipped_0 = flip_h(sum_banks, "sum", xn_tiles[0:GROUP_TILES])
+        scale_h(0, flipped_0)
+        flipped_1 = flip_h(flip_banks, "flip", xn_tiles[GROUP_TILES:TOKEN_TILES])
+        pack_h(0)
+        scale_h(1, flipped_1)
+
+        sums_0 = multiply(0, group_tiles[0])
+        ready[1] = flip_and_copy_weights(1)
+        pack_h(1)
+        finish(0, group_tiles[0], sums_0)
+        sums_1 = multiply(0, group_tiles[1])
+        for g in range(PASSES):
+            quantise_weights(1, g, ready[1][g])
+        ready[2] = flip_and_copy_weights(2)
+        finish(0, group_tiles[1], sums_1)
+
+        for c in range(1, CHUNKS):
+            sums = multiply(c, all_tiles)
+            if c + 1 < CHUNKS:
+                for g in range(PASSES):
+                    quantise_weights(c + 1, g, ready[c + 1][g])
+            if c + 2 < CHUNKS:
+                ready[c + 2] = flip_and_copy_weights(c + 2)
+            finish(c, all_tiles, sums)

@@ -25,14 +25,15 @@ K_BLOCK = P * PAIR
 K_BLOCKS = D // K_BLOCK
 
 TOKEN_TILES = TOKENS // P
-GROUP_TILES = 2
-TOKEN_GROUP = GROUP_TILES * P
+TOKEN_GROUP = 2 * P
 TOKEN_GROUPS = TOKENS // TOKEN_GROUP
 
 CHUNK = 512
 CHUNKS = FEATURES // CHUNK
 ROW_TILES = CHUNK // P
-BANK_ROW_TILES = 2
+AHEAD = 4
+
+RUN = 4
 
 BN_WIDTH = 512
 BN_OUT = 6
@@ -46,12 +47,11 @@ def tile_block_pa_kernel(tc, x, W_qkv, b_qkv, g1, beta1, out_0, out_1, out_2):
     out_rows = [o.rearrange("b t h d -> (b t) (h d)") for o in (out_0, out_1, out_2)]
 
     with ExitStack() as ctx:
-        ctx.enter_context(tc.manual_schedule())
         keep = ctx.enter_context(tc.tile_pool(name="keep", bufs=1))
         small = ctx.enter_context(tc.tile_pool(name="small", bufs=TOKEN_TILES))
         normed = ctx.enter_context(tc.tile_pool(name="normed", bufs=TOKEN_TILES))
-        grouped = ctx.enter_context(tc.tile_pool(name="grouped", bufs=2 * PASSES))
-        results = ctx.enter_context(tc.tile_pool(name="results", bufs=2 * TOKEN_TILES))
+        grouped = ctx.enter_context(tc.tile_pool(name="grouped", bufs=PASSES * AHEAD))
+        results = ctx.enter_context(tc.tile_pool(name="results", bufs=8))
         flip_banks = ctx.enter_context(tc.psum_pool(name="flip_banks", bufs=4))
         sum_banks = ctx.enter_context(tc.psum_pool(name="sum_banks", bufs=4))
 
@@ -64,6 +64,11 @@ def tile_block_pa_kernel(tc, x, W_qkv, b_qkv, g1, beta1, out_0, out_1, out_2):
             out=gain_rows[K_BLOCKS : 2 * K_BLOCKS, :],
             in_=beta1.rearrange("(r c) -> r c", c=K_BLOCK),
         )
+        bias_rows = keep.tile([P, CHUNK], BF16)
+        nc.vector.memset(bias_rows[:], 0.0)
+        nc.sync.dma_start(
+            out=bias_rows[0:CHUNKS, :], in_=b_qkv.rearrange("(r c) -> r c", c=CHUNK)
+        )
         x_sb = keep.tile([P, TOKEN_TILES, D], BF16)
         for i in range(TOKEN_TILES):
             nc.sync.dma_start(out=x_sb[:, i, :], in_=x_rows[i * P : (i + 1) * P, :])
@@ -74,14 +79,37 @@ def tile_block_pa_kernel(tc, x, W_qkv, b_qkv, g1, beta1, out_0, out_1, out_2):
                 in_=W_qkv[c * CHUNK : (c + 1) * CHUNK, :].rearrange("(r p) k -> p r k", p=P),
             )
         w_words = w_sb[:].bitcast(F32)
-        bias_all = keep.tile([P, FEATURES], BF16)
 
         eps_col = keep.tile([P, 1], F32)
         nc.vector.memset(eps_col[:], LN_EPS)
         table_warmer = keep.tile([P, 1], F32)
         nc.scalar.activation(out=table_warmer[:], in_=eps_col[:], func=ACT.Sqrt)
-        ident = keep.tile([P, P], F32)
-        make_identity(nc, ident[:])
+        ident_f32 = keep.tile([P, P], F32)
+        make_identity(nc, ident_f32[:])
+        ident_bf16 = keep.tile([P, P], BF16)
+        make_identity(nc, ident_bf16[:])
+
+        gain_flipped = flip_banks.tile([P, P], F32, tag="flip")
+        nc.tensor.transpose(gain_flipped[:], gain_rows[:].bitcast(F32), ident_f32[:])
+        gain_pairs = keep.tile([P, 2 * K_BLOCKS], F32)
+        nc.vector.tensor_copy(out=gain_pairs[:], in_=gain_flipped[:, 0 : 2 * K_BLOCKS])
+        gain_cols = keep.tile([P, 2 * K_BLOCKS * PAIR], F32)
+        nc.vector.tensor_copy(out=gain_cols[:], in_=gain_pairs[:].bitcast(BF16))
+        beta_at = K_BLOCKS * PAIR
+
+        bias_all = keep.tile([P, FEATURES], BF16)
+        for b in range(CHUNKS // 2):
+            bias_bank = flip_banks.tile([P, 2 * CHUNK], BF16, tag="flip")
+            for half in range(2):
+                c = 2 * b + half
+                nc.tensor.matmul(
+                    out=bias_bank[:, half * CHUNK : (half + 1) * CHUNK],
+                    lhsT=ident_bf16[:, c : c + 1].to_broadcast([P, P]),
+                    rhs=bias_rows[:],
+                    start=True,
+                    stop=True,
+                )
+            nc.scalar.copy(out=bias_all[:, 2 * b * CHUNK : 2 * (b + 1) * CHUNK], in_=bias_bank[:])
 
         h_codes = keep.tile([P, PASSES, TOKENS], U32, align_bytes=64)
         h_scales = keep.tile([P, PASSES, TOKENS], U8, align_bytes=64)
@@ -89,17 +117,8 @@ def tile_block_pa_kernel(tc, x, W_qkv, b_qkv, g1, beta1, out_0, out_1, out_2):
         w_scales = keep.tile([P, CHUNKS, PASSES, CHUNK], U8, align_bytes=64)
         h_planes = keep.tile([P, PASSES, PACK, TOKENS], BF16)
         h_grouped = keep.tile([P, PASSES, TOKENS, PACK], BF16, align_bytes=64)
-        gain_cols = keep.tile([P, 2 * K_BLOCKS * PAIR], F32)
-        beta_at = K_BLOCKS * PAIR
 
-        def spread_gains():
-            gain_flipped = flip_banks.tile([P, P], F32, tag="flip")
-            nc.tensor.transpose(gain_flipped[:], gain_rows[:].bitcast(F32), ident[:])
-            gain_pairs = keep.tile([P, 2 * K_BLOCKS], F32)
-            nc.vector.tensor_copy(out=gain_pairs[:], in_=gain_flipped[:, 0 : 2 * K_BLOCKS])
-            nc.vector.tensor_copy(out=gain_cols[:], in_=gain_pairs[:].bitcast(BF16))
-
-        def statistics(i):
+        def normalise(i):
             stats = small.tile([P, D // BN_WIDTH, BN_OUT], F32)
             for s in range(D // BN_WIDTH):
                 nc.vector.bn_stats(
@@ -107,15 +126,12 @@ def tile_block_pa_kernel(tc, x, W_qkv, b_qkv, g1, beta1, out_0, out_1, out_2):
                 )
             mean_var = small.tile([P, 2], F32)
             nc.vector.bn_aggr(out=mean_var[:], in_=stats[:].rearrange("p s d -> p (s d)"))
-            neg_mean = small.tile([P, 1], F32)
-            nc.vector.tensor_scalar_mul(out=neg_mean[:], in0=mean_var[:, 0:1], scalar1=-1.0)
             std = small.tile([P, 1], F32)
             nc.scalar.activation(out=std[:], in_=mean_var[:, 1:2], func=ACT.Sqrt, bias=eps_col[:])
-            return neg_mean, std
-
-        def normalise(i, neg_mean, std):
             rstd = small.tile([P, 1], F32)
             nc.vector.reciprocal(out=rstd[:], in_=std[:])
+            neg_mean = small.tile([P, 1], F32)
+            nc.vector.tensor_scalar_mul(out=neg_mean[:], in0=mean_var[:, 0:1], scalar1=-1.0)
             xn = normed.tile([P, PAIR, D // PAIR], F32)
             nc.gpsimd.tensor_scalar(
                 out=xn[:],
@@ -127,38 +143,41 @@ def tile_block_pa_kernel(tc, x, W_qkv, b_qkv, g1, beta1, out_0, out_1, out_2):
             )
             return xn
 
-        def flip_h(banks, tag, xn_tiles):
-            flipped = []
-            for b in range(K_BLOCKS):
-                bank = banks.tile([P, PAIR, TOKEN_GROUP], F32, tag=tag)
-                for r, xn in enumerate(xn_tiles):
-                    for e in range(PAIR):
-                        nc.tensor.transpose(
-                            bank[:, e, r * P : (r + 1) * P], xn[:, e, b * P : (b + 1) * P], ident[:]
-                        )
-                flipped.append(bank)
-            return flipped
-
-        def scale_h(group, flipped):
+        def quantise_h(group, xn_tiles):
             tokens = slice(group * TOKEN_GROUP, (group + 1) * TOKEN_GROUP)
             for b in range(K_BLOCKS):
                 g, u = divmod(b, 2)
+                flipped = sum_banks.tile([P, PAIR, TOKEN_GROUP], F32, tag="sum")
+                for r, xn in enumerate(xn_tiles):
+                    for e in range(PAIR):
+                        nc.tensor.transpose(
+                            flipped[:, e, r * P : (r + 1) * P],
+                            xn[:, e, b * P : (b + 1) * P],
+                            ident_f32[:],
+                        )
                 for e in range(PAIR):
                     col = PAIR * b + e
-                    nc.scalar.activation(
-                        out=h_planes[:, g, PAIR * u + e, tokens],
-                        in_=flipped[b][:, e, :],
-                        func=ACT.Identity,
-                        scale=gain_cols[:, col : col + 1],
-                        bias=gain_cols[:, beta_at + col : beta_at + col + 1],
-                    )
-
-        def pack_h(group):
-            tokens = slice(group * TOKEN_GROUP, (group + 1) * TOKEN_GROUP)
+                    if b % 2 == 0:
+                        nc.scalar.activation(
+                            out=h_planes[:, g, PAIR * u + e, tokens],
+                            in_=flipped[:, e, :],
+                            func=ACT.Identity,
+                            scale=gain_cols[:, col : col + 1],
+                            bias=gain_cols[:, beta_at + col : beta_at + col + 1],
+                        )
+                    else:
+                        nc.vector.tensor_scalar(
+                            out=h_planes[:, g, PAIR * u + e, tokens],
+                            in0=flipped[:, e, :],
+                            scalar1=gain_cols[:, col : col + 1],
+                            scalar2=gain_cols[:, beta_at + col : beta_at + col + 1],
+                            op0=ALU.mult,
+                            op1=ALU.add,
+                        )
             for g in range(PASSES):
                 nc.vector.tensor_copy(
-                    out=h_grouped[:, g, tokens, :],
-                    in_=h_planes[:, g, :, tokens].rearrange("p t n -> p n t"),
+                    out=h_grouped[:, g, tokens, :].rearrange("p (c i) t -> p c t i", i=RUN),
+                    in_=h_planes[:, g, :, tokens].rearrange("p t (c i) -> p c t i", i=RUN),
                 )
             for g in range(PASSES):
                 nc.vector.quantize_mx(
@@ -167,45 +186,35 @@ def tile_block_pa_kernel(tc, x, W_qkv, b_qkv, g1, beta1, out_0, out_1, out_2):
                     in_=h_grouped[:, g, tokens, :].rearrange("p n t -> p (n t)"),
                 )
 
-        def flip_weights(c, g):
-            flipped = []
-            for half in range(ROW_TILES // BANK_ROW_TILES):
-                bank = flip_banks.tile([P, BANK_ROW_TILES, 2, P], F32, tag="flip")
-                for r in range(BANK_ROW_TILES):
-                    for u in range(2):
-                        b = 2 * g + u
-                        nc.tensor.transpose(
-                            bank[:, r, u, :],
-                            w_words[:, c, BANK_ROW_TILES * half + r, b * P : (b + 1) * P],
-                            ident[:],
-                        )
-                flipped.append(bank)
-            return flipped
-
-        def copy_weights(flipped):
-            w_grouped = grouped.tile([P, CHUNK * PACK], BF16, align_bytes=64)
-            w_grouped_words = w_grouped[:].bitcast(F32).rearrange(
-                "p (r f u) -> p r f u", r=ROW_TILES, u=2
-            )
-            for half, bank in enumerate(flipped):
-                nc.scalar.copy(
-                    out=w_grouped_words[
-                        :, BANK_ROW_TILES * half : BANK_ROW_TILES * (half + 1), :, :
-                    ],
-                    in_=bank[:].rearrange("p r u f -> p r f u"),
+        def prepare_weights(c):
+            for g in range(PASSES):
+                w_grouped = grouped.tile([P, CHUNK * PACK], BF16, align_bytes=64)
+                w_grouped_words = w_grouped[:].bitcast(F32).rearrange(
+                    "p (r f u) -> p r f u", r=ROW_TILES, u=2
                 )
-            return w_grouped
+                for half in range(2):
+                    flipped = flip_banks.tile([P, 2, 2, P], F32, tag="flip")
+                    for r in range(2):
+                        for u in range(2):
+                            b = 2 * g + u
+                            nc.tensor.transpose(
+                                flipped[:, r, u, :],
+                                w_words[:, c, 2 * half + r, b * P : (b + 1) * P],
+                                ident_f32[:],
+                            )
+                    nc.scalar.copy(
+                        out=w_grouped_words[:, 2 * half : 2 * half + 2, :, :],
+                        in_=flipped[:].rearrange("p r u f -> p r f u"),
+                    )
+                nc.vector.quantize_mx(
+                    out=w_codes[:, c, g, :].bitcast(FP8X4),
+                    scales=w_scales[:, c, g, :],
+                    in_=w_grouped[:],
+                )
 
-        def quantise_weights(c, g, w_grouped):
-            nc.vector.quantize_mx(
-                out=w_codes[:, c, g, :].bitcast(FP8X4),
-                scales=w_scales[:, c, g, :],
-                in_=w_grouped[:],
-            )
-
-        def multiply(c, tiles):
-            banks = []
-            for i in tiles:
+        def multiply(c):
+            columns = slice((c % 2) * CHUNK, (c % 2 + 1) * CHUNK)
+            for i in range(TOKEN_TILES):
                 rows = slice(i * P, (i + 1) * P)
                 sums = sum_banks.tile([P, CHUNK], F32, tag="sum")
                 for g in range(PASSES):
@@ -218,12 +227,6 @@ def tile_block_pa_kernel(tc, x, W_qkv, b_qkv, g1, beta1, out_0, out_1, out_2):
                         start=(g == 0),
                         stop=(g == PASSES - 1),
                     )
-                banks.append(sums)
-            return banks
-
-        def finish(c, tiles, banks):
-            columns = slice((c % 2) * CHUNK, (c % 2 + 1) * CHUNK)
-            for i, sums in zip(tiles, banks):
                 result = results.tile([P, CHUNK], F32)
                 nc.vector.tensor_tensor(
                     out=result[:],
@@ -231,56 +234,14 @@ def tile_block_pa_kernel(tc, x, W_qkv, b_qkv, g1, beta1, out_0, out_1, out_2):
                     in1=bias_all[:, c * CHUNK : (c + 1) * CHUNK],
                     op=ALU.add,
                 )
-                nc.sync.dma_start(
-                    out=out_rows[c // 2][i * P : (i + 1) * P, columns], in_=result[:]
-                )
+                nc.sync.dma_start(out=out_rows[c // 2][rows, columns], in_=result[:])
 
-        def flip_and_copy_weights(c):
-            flipped = [flip_weights(c, g) for g in range(PASSES)]
-            return [copy_weights(banks) for banks in flipped]
-
-        group_tiles = [
-            list(range(q * GROUP_TILES, (q + 1) * GROUP_TILES)) for q in range(TOKEN_GROUPS)
-        ]
-        all_tiles = list(range(TOKEN_TILES))
-
-        moments = []
-        xn_tiles = []
-        ready = {}
-        ready[0] = []
-        for i in range(TOKEN_TILES):
-            moments.append(statistics(i))
-            if i >= 1:
-                xn_tiles.append(normalise(i - 1, *moments[i - 1]))
-            if i >= TOKEN_TILES - PASSES:
-                ready[0].append(copy_weights(flip_weights(0, i - (TOKEN_TILES - PASSES))))
-        xn_tiles.append(normalise(TOKEN_TILES - 1, *moments[TOKEN_TILES - 1]))
-        spread_gains()
-        nc.scalar.dma_start(out=bias_all[:], in_=b_qkv.partition_broadcast(P))
-        for g in range(PASSES):
-            quantise_weights(0, g, ready[0][g])
-
-        flipped_0 = flip_h(sum_banks, "sum", xn_tiles[0:GROUP_TILES])
-        scale_h(0, flipped_0)
-        flipped_1 = flip_h(flip_banks, "flip", xn_tiles[GROUP_TILES:TOKEN_TILES])
-        pack_h(0)
-        scale_h(1, flipped_1)
-
-        sums_0 = multiply(0, group_tiles[0])
-        ready[1] = flip_and_copy_weights(1)
-        pack_h(1)
-        finish(0, group_tiles[0], sums_0)
-        sums_1 = multiply(0, group_tiles[1])
-        for g in range(PASSES):
-            quantise_weights(1, g, ready[1][g])
-        ready[2] = flip_and_copy_weights(2)
-        finish(0, group_tiles[1], sums_1)
-
-        for c in range(1, CHUNKS):
-            sums = multiply(c, all_tiles)
-            if c + 1 < CHUNKS:
-                for g in range(PASSES):
-                    quantise_weights(c + 1, g, ready[c + 1][g])
-            if c + 2 < CHUNKS:
-                ready[c + 2] = flip_and_copy_weights(c + 2)
-            finish(c, all_tiles, sums)
+        for group in range(TOKEN_GROUPS):
+            quantise_h(group, [normalise(2 * group), normalise(2 * group + 1)])
+            prepare_weights(group)
+        for c in range(TOKEN_GROUPS, AHEAD):
+            prepare_weights(c)
+        for c in range(CHUNKS):
+            if c + AHEAD < CHUNKS:
+                prepare_weights(c + AHEAD)
+            multiply(c)

from contextlib import ExitStack

import concourse.mybir as mybir
from concourse.masks import make_identity

F32 = mybir.dt.float32
BF16 = mybir.dt.bfloat16
U32 = mybir.dt.uint32
U8 = mybir.dt.uint8
FP8X4 = mybir.dt.float8_e4m3fn_x4
ACT = mybir.ActivationFunctionType
ALU = mybir.AluOpType

P = 128
TOKENS = 512
D = 1024
FEATURES = 3 * D
LN_EPS = 1e-6

PACK = 4
K_PASS = P * PACK
PASSES = D // K_PASS
PAIR = 2
K_BLOCK = P * PAIR
K_BLOCKS = D // K_BLOCK

TOKEN_TILES = TOKENS // P
TOKEN_GROUP = 2 * P
TOKEN_GROUPS = TOKENS // TOKEN_GROUP

CHUNK = 512
CHUNKS = FEATURES // CHUNK
ROW_TILES = CHUNK // P
AHEAD = 4

RUN = 4

BN_WIDTH = 512
BN_OUT = 6

FLOPS = 2 * TOKENS * D * FEATURES


def tile_block_pa_kernel(tc, x, W_qkv, b_qkv, g1, beta1, out_0, out_1, out_2):
    nc = tc.nc
    x_rows = x.flatten_outer_dims()
    out_rows = [o.rearrange("b t h d -> (b t) (h d)") for o in (out_0, out_1, out_2)]

    with ExitStack() as ctx:
        keep = ctx.enter_context(tc.tile_pool(name="keep", bufs=1))
        small = ctx.enter_context(tc.tile_pool(name="small", bufs=TOKEN_TILES))
        normed = ctx.enter_context(tc.tile_pool(name="normed", bufs=TOKEN_TILES))
        grouped = ctx.enter_context(tc.tile_pool(name="grouped", bufs=PASSES * AHEAD))
        results = ctx.enter_context(tc.tile_pool(name="results", bufs=8))
        flip_banks = ctx.enter_context(tc.psum_pool(name="flip_banks", bufs=4))
        sum_banks = ctx.enter_context(tc.psum_pool(name="sum_banks", bufs=4))

        gain_rows = keep.tile([P, K_BLOCK], BF16)
        nc.vector.memset(gain_rows[:], 0.0)
        nc.sync.dma_start(
            out=gain_rows[0:K_BLOCKS, :], in_=g1.rearrange("(r c) -> r c", c=K_BLOCK)
        )
        nc.sync.dma_start(
            out=gain_rows[K_BLOCKS : 2 * K_BLOCKS, :],
            in_=beta1.rearrange("(r c) -> r c", c=K_BLOCK),
        )
        bias_rows = keep.tile([P, CHUNK], BF16)
        nc.vector.memset(bias_rows[:], 0.0)
        nc.sync.dma_start(
            out=bias_rows[0:CHUNKS, :], in_=b_qkv.rearrange("(r c) -> r c", c=CHUNK)
        )
        x_sb = keep.tile([P, TOKEN_TILES, D], BF16)
        for i in range(TOKEN_TILES):
            nc.sync.dma_start(out=x_sb[:, i, :], in_=x_rows[i * P : (i + 1) * P, :])
        w_sb = keep.tile([P, CHUNKS, ROW_TILES, D], BF16)
        for c in range(CHUNKS):
            nc.sync.dma_start(
                out=w_sb[:, c, :, :],
                in_=W_qkv[c * CHUNK : (c + 1) * CHUNK, :].rearrange("(r p) k -> p r k", p=P),
            )
        w_words = w_sb[:].bitcast(F32)

        eps_col = keep.tile([P, 1], F32)
        nc.vector.memset(eps_col[:], LN_EPS)
        table_warmer = keep.tile([P, 1], F32)
        nc.scalar.activation(out=table_warmer[:], in_=eps_col[:], func=ACT.Sqrt)
        ident_f32 = keep.tile([P, P], F32)
        make_identity(nc, ident_f32[:])
        ident_bf16 = keep.tile([P, P], BF16)
        make_identity(nc, ident_bf16[:])

        gain_flipped = flip_banks.tile([P, P], F32, tag="flip")
        nc.tensor.transpose(gain_flipped[:], gain_rows[:].bitcast(F32), ident_f32[:])
        gain_pairs = keep.tile([P, 2 * K_BLOCKS], F32)
        nc.vector.tensor_copy(out=gain_pairs[:], in_=gain_flipped[:, 0 : 2 * K_BLOCKS])
        gain_cols = keep.tile([P, 2 * K_BLOCKS * PAIR], F32)
        nc.vector.tensor_copy(out=gain_cols[:], in_=gain_pairs[:].bitcast(BF16))
        beta_at = K_BLOCKS * PAIR

        bias_all = keep.tile([P, FEATURES], BF16)
        for b in range(CHUNKS // 2):
            bias_bank = flip_banks.tile([P, 2 * CHUNK], BF16, tag="flip")
            for half in range(2):
                c = 2 * b + half
                nc.tensor.matmul(
                    out=bias_bank[:, half * CHUNK : (half + 1) * CHUNK],
                    lhsT=ident_bf16[:, c : c + 1].to_broadcast([P, P]),
                    rhs=bias_rows[:],
                    start=True,
                    stop=True,
                )
            nc.scalar.copy(out=bias_all[:, 2 * b * CHUNK : 2 * (b + 1) * CHUNK], in_=bias_bank[:])

        h_codes = keep.tile([P, PASSES, TOKENS], U32, align_bytes=64)
        h_scales = keep.tile([P, PASSES, TOKENS], U8, align_bytes=64)
        w_codes = keep.tile([P, CHUNKS, PASSES, CHUNK], U32, align_bytes=64)
        w_scales = keep.tile([P, CHUNKS, PASSES, CHUNK], U8, align_bytes=64)
        h_planes = keep.tile([P, PASSES, PACK, TOKENS], BF16)
        h_grouped = keep.tile([P, PASSES, TOKENS, PACK], BF16, align_bytes=64)

        def normalise(i):
            stats = small.tile([P, D // BN_WIDTH, BN_OUT], F32)
            for s in range(D // BN_WIDTH):
                nc.vector.bn_stats(
                    out=stats[:, s, :], in_=x_sb[:, i, s * BN_WIDTH : (s + 1) * BN_WIDTH]
                )
            mean_var = small.tile([P, 2], F32)
            nc.vector.bn_aggr(out=mean_var[:], in_=stats[:].rearrange("p s d -> p (s d)"))
            std = small.tile([P, 1], F32)
            nc.scalar.activation(out=std[:], in_=mean_var[:, 1:2], func=ACT.Sqrt, bias=eps_col[:])
            rstd = small.tile([P, 1], F32)
            nc.vector.reciprocal(out=rstd[:], in_=std[:])
            neg_mean = small.tile([P, 1], F32)
            nc.vector.tensor_scalar_mul(out=neg_mean[:], in0=mean_var[:, 0:1], scalar1=-1.0)
            xn = normed.tile([P, PAIR, D // PAIR], F32)
            nc.gpsimd.tensor_scalar(
                out=xn[:],
                in0=x_sb[:, i, :].rearrange("p (j e) -> p e j", e=PAIR),
                scalar1=neg_mean[:],
                scalar2=rstd[:],
                op0=ALU.add,
                op1=ALU.mult,
            )
            return xn

        def quantise_h(group, xn_tiles):
            tokens = slice(group * TOKEN_GROUP, (group + 1) * TOKEN_GROUP)
            for b in range(K_BLOCKS):
                g, u = divmod(b, 2)
                flipped = sum_banks.tile([P, PAIR, TOKEN_GROUP], F32, tag="sum")
                for r, xn in enumerate(xn_tiles):
                    for e in range(PAIR):
                        nc.tensor.transpose(
                            flipped[:, e, r * P : (r + 1) * P],
                            xn[:, e, b * P : (b + 1) * P],
                            ident_f32[:],
                        )
                for e in range(PAIR):
                    col = PAIR * b + e
                    if b % 2 == 0:
                        nc.scalar.activation(
                            out=h_planes[:, g, PAIR * u + e, tokens],
                            in_=flipped[:, e, :],
                            func=ACT.Identity,
                            scale=gain_cols[:, col : col + 1],
                            bias=gain_cols[:, beta_at + col : beta_at + col + 1],
                        )
                    else:
                        nc.vector.tensor_scalar(
                            out=h_planes[:, g, PAIR * u + e, tokens],
                            in0=flipped[:, e, :],
                            scalar1=gain_cols[:, col : col + 1],
                            scalar2=gain_cols[:, beta_at + col : beta_at + col + 1],
                            op0=ALU.mult,
                            op1=ALU.add,
                        )
            for g in range(PASSES):
                nc.vector.tensor_copy(
                    out=h_grouped[:, g, tokens, :].rearrange("p (c i) t -> p c t i", i=RUN),
                    in_=h_planes[:, g, :, tokens].rearrange("p t (c i) -> p c t i", i=RUN),
                )
            for g in range(PASSES):
                nc.vector.quantize_mx(
                    out=h_codes[:, g, tokens].bitcast(FP8X4),
                    scales=h_scales[:, g, tokens],
                    in_=h_grouped[:, g, tokens, :].rearrange("p n t -> p (n t)"),
                )

        def prepare_weights(c):
            for g in range(PASSES):
                w_grouped = grouped.tile([P, CHUNK * PACK], BF16, align_bytes=64)
                w_grouped_words = w_grouped[:].bitcast(F32).rearrange(
                    "p (r f u) -> p r f u", r=ROW_TILES, u=2
                )
                for half in range(2):
                    flipped = flip_banks.tile([P, 2, 2, P], F32, tag="flip")
                    for r in range(2):
                        for u in range(2):
                            b = 2 * g + u
                            nc.tensor.transpose(
                                flipped[:, r, u, :],
                                w_words[:, c, 2 * half + r, b * P : (b + 1) * P],
                                ident_f32[:],
                            )
                    nc.scalar.copy(
                        out=w_grouped_words[:, 2 * half : 2 * half + 2, :, :],
                        in_=flipped[:].rearrange("p r u f -> p r f u"),
                    )
                nc.vector.quantize_mx(
                    out=w_codes[:, c, g, :].bitcast(FP8X4),
                    scales=w_scales[:, c, g, :],
                    in_=w_grouped[:],
                )

        def multiply(c):
            columns = slice((c % 2) * CHUNK, (c % 2 + 1) * CHUNK)
            for i in range(TOKEN_TILES):
                rows = slice(i * P, (i + 1) * P)
                sums = sum_banks.tile([P, CHUNK], F32, tag="sum")
                for g in range(PASSES):
                    nc.tensor.matmul_mx(
                        out=sums[:],
                        lhsT=h_codes[:, g, rows].bitcast(FP8X4),
                        lhsT_scale=h_scales[:, g, rows],
                        rhs=w_codes[:, c, g, :].bitcast(FP8X4),
                        rhs_scale=w_scales[:, c, g, :],
                        start=(g == 0),
                        stop=(g == PASSES - 1),
                    )
                result = results.tile([P, CHUNK], F32)
                nc.vector.tensor_tensor(
                    out=result[:],
                    in0=sums[:],
                    in1=bias_all[:, c * CHUNK : (c + 1) * CHUNK],
                    op=ALU.add,
                )
                nc.sync.dma_start(out=out_rows[c // 2][rows, columns], in_=result[:])

        for group in range(TOKEN_GROUPS):
            quantise_h(group, [normalise(2 * group), normalise(2 * group + 1)])
            prepare_weights(group)
        for c in range(TOKEN_GROUPS, AHEAD):
            prepare_weights(c)
        for c in range(CHUNKS):
            if c + AHEAD < CHUNKS:
                prepare_weights(c + AHEAD)
            multiply(c)
